import numpy as np
import ml_dtypes


def mxq(x, axis, fmt="e4m3"):
    dtype, down = {"e4m3": (ml_dtypes.float8_e4m3fn, 7), "e5m2": (ml_dtypes.float8_e5m2, 14)}[fmt]
    v = np.moveaxis(np.asarray(x, np.float32).astype(ml_dtypes.bfloat16).astype(np.float64), axis, -1)
    blocks = v.reshape(v.shape[:-1] + (-1, 32))
    amax = np.abs(blocks).max(-1, keepdims=True)
    byte = np.maximum(np.where(amax > 0, np.frexp(amax)[1] - 1 + 127, 0) - down, 1)
    scale = np.exp2(byte - 127.0)
    codes = (blocks / scale).astype(np.float32).astype(dtype).astype(np.float64)
    return np.moveaxis((codes * scale).reshape(v.shape), -1, axis)


WIDE = False


def mx_kscale(k):
    if not WIDE:
        return np.ones(k)
    levels = np.array([10, -10, 5, -5, 0])
    if k % 512:
        return np.exp2(np.random.permutation(np.resize(levels, k // 32))).repeat(32)
    a = np.empty((k // 512, 16))
    for p in range(k // 512):
        a[p, :8] = np.random.permutation(np.resize(levels, 8))
        for g in range(8):
            far = levels[np.abs(levels - a[p, g]) >= 10]
            a[p, g + 8] = far[np.random.randint(len(far))]
    return np.exp2(a.ravel()).repeat(32)


BF16 = ml_dtypes.bfloat16


def bf(x):
    return np.asarray(x, np.float32).astype(BF16)


def f64(x):
    return np.asarray(x).astype(np.float64)


N, D_IN, D_HID, D_OUT = 512, 512, 512, 512


def hamilton_Wq(Wr, Wi, Wj, Wk, xr, xi, xj, xk):
    x_cat = np.concatenate([xr, xi, xj, xk], axis=-1)
    n_in = Wr.shape[1]
    Wq = mxq(np.concatenate([Wr, Wi, Wj, Wk], axis=1), 1, "e4m3")
    Wr, Wi, Wj, Wk = Wq[:, :n_in], Wq[:, n_in:2 * n_in], Wq[:, 2 * n_in:3 * n_in], Wq[:, 3 * n_in:]
    W_block = np.concatenate([
        np.concatenate([Wr, Wi, Wj, Wk], axis=0),
        np.concatenate([-Wi, Wr, -Wk, Wj], axis=0),
        np.concatenate([-Wj, Wk, Wr, -Wi], axis=0),
        np.concatenate([-Wk, -Wj, Wi, Wr], axis=0),
    ], axis=1)
    h = mxq(x_cat, 1, "e4m3") @ W_block.T
    out = Wr.shape[0]
    return h[:, :out], h[:, out:2 * out], h[:, 2 * out:3 * out], h[:, 3 * out:]


def setup_inputs():
    s = mx_kscale(4 * D_IN)[:D_IN]
    t = mx_kscale(4 * D_HID)[:D_HID]
    inp = {}
    for c in "rijk":
        inp["q_" + c] = bf(np.random.standard_normal((N, D_IN)) * s)
    for c in "rijk":
        inp["W1_" + c] = bf(np.random.standard_normal((D_HID, D_IN)) * 0.5 / np.sqrt(D_IN) / s[None, :] * t[:, None])
    for c in "rijk":
        inp["b1_" + c] = bf(((0.0 if c == "r" else 0.2) + 0.1 * np.random.standard_normal(D_HID)) * t)
    for c in "rijk":
        inp["W2_" + c] = bf(np.random.standard_normal((D_OUT, D_HID)) * 0.7 / np.sqrt(D_HID) / t[None, :])
    for c in "rijk":
        inp["b2_" + c] = bf((0.0 if c == "r" else 0.2) + 0.1 * np.random.standard_normal(D_OUT))
    return inp


def reference(q_r, q_i, q_j, q_k,
              W1_r, W1_i, W1_j, W1_k, b1_r, b1_i, b1_j, b1_k,
              W2_r, W2_i, W2_j, W2_k, b2_r, b2_i, b2_j, b2_k):
    hr, hi, hj, hk = hamilton_Wq(f64(W1_r), f64(W1_i), f64(W1_j), f64(W1_k), f64(q_r), f64(q_i), f64(q_j), f64(q_k))
    hr = np.maximum(hr + f64(b1_r), 0.0)
    hi = np.maximum(hi + f64(b1_i), 0.0)
    hj = np.maximum(hj + f64(b1_j), 0.0)
    hk = np.maximum(hk + f64(b1_k), 0.0)
    or_, oi, oj, ok = hamilton_Wq(f64(W2_r), f64(W2_i), f64(W2_j), f64(W2_k), hr, hi, hj, hk)
    return (or_ + f64(b2_r), oi + f64(b2_i), oj + f64(b2_j), ok + f64(b2_k))

@@ -1,0 +1,238 @@
+from contextlib import ExitStack
+
+import concourse.mybir as mybir
+from concourse.masks import make_identity
+
+F32 = mybir.dt.float32
+BF16 = mybir.dt.bfloat16
+U32 = mybir.dt.uint32
+U8 = mybir.dt.uint8
+FP8X4 = mybir.dt.float8_e4m3fn_x4
+
+P = 128
+SIZE = 512
+TILES = SIZE // P
+PACK = 4
+PARTS = 4
+
+FLOPS = 2 * 2 * SIZE * (PARTS * SIZE) * (PARTS * SIZE)
+
+HAMILTON = (
+    ((0, 1), (1, -1), (2, -1), (3, -1)),
+    ((1, 1), (0, 1), (3, 1), (2, -1)),
+    ((2, 1), (3, -1), (0, 1), (1, 1)),
+    ((3, 1), (2, 1), (1, -1), (0, 1)),
+)
+
+
+def tile_qmlp_kernel(
+    tc,
+    q_r, q_i, q_j, q_k,
+    W1_r, W1_i, W1_j, W1_k,
+    b1_r, b1_i, b1_j, b1_k,
+    W2_r, W2_i, W2_j, W2_k,
+    b2_r, b2_i, b2_j, b2_k,
+    out_0, out_1, out_2, out_3,
+):
+    nc = tc.nc
+    q = (q_r, q_i, q_j, q_k)
+    w1 = (W1_r, W1_i, W1_j, W1_k)
+    b1 = (b1_r, b1_i, b1_j, b1_k)
+    w2 = (W2_r, W2_i, W2_j, W2_k)
+    b2 = (b2_r, b2_i, b2_j, b2_k)
+    outs = (out_0, out_1, out_2, out_3)
+
+    with ExitStack() as ctx:
+        const = ctx.enter_context(tc.tile_pool(name="const", bufs=1))
+        raw_pool = ctx.enter_context(tc.tile_pool(name="raw", bufs=1))
+        grouped_pool = ctx.enter_context(tc.tile_pool(name="grouped", bufs=8))
+        planar_pool = ctx.enter_context(tc.tile_pool(name="planar", bufs=2))
+        mx_pool = ctx.enter_context(tc.tile_pool(name="mx", bufs=1))
+        result_pool = ctx.enter_context(tc.tile_pool(name="result", bufs=4))
+        psum = ctx.enter_context(tc.psum_pool(name="psum", bufs=8))
+        ctx.enter_context(tc.manual_schedule())
+
+        def load(name, view):
+            raw = raw_pool.tile([P, TILES * SIZE], BF16, name=name)
+            nc.sync.dma_start(out=raw[:].rearrange("p (n x) -> p n x", n=view.shape[1]), in_=view)
+            return raw
+
+        q_raw = []
+        w1_raw = []
+        for c in range(PARTS):
+            w1_raw.append(load("w1_raw%d" % c, w1[c].rearrange("(p t) k -> p t k", t=TILES)))
+            q_raw.append(load("q_raw%d" % c, q[c].rearrange("(p a) k -> p a k", a=TILES)))
+        b1_sb = const.tile([P, PARTS, 16], BF16, name="b1_sb")
+        for c in range(PARTS):
+            nc.sync.dma_start(
+                out=b1_sb[:, c, 0:TILES],
+                in_=b1[c].rearrange("(p t) -> p t", t=TILES),
+            )
+        w2_raw = [
+            load("w2_raw%d" % c, w2[c].rearrange("(a p) k -> p a k", p=P)) for c in range(PARTS)
+        ]
+        b2_sb = const.tile([P, PARTS, SIZE], BF16, name="b2_sb")
+        for c in range(PARTS):
+            nc.sync.dma_start(out=b2_sb[:, c, :], in_=b2[c].partition_broadcast(P))
+
+        ident = const.tile([P, P], F32, name="ident")
+        make_identity(nc, ident[:])
+
+        def transpose_component(raw, name):
+            words = raw[:].bitcast(F32)
+            grouped = grouped_pool.tile(
+                [P, SIZE * PACK], BF16, name=name, tag="grouped", align_bytes=64
+            )
+            grouped_words = grouped[:].bitcast(F32)
+            half = SIZE
+            for b in range(2):
+                bank = psum.tile([P, SIZE], F32, name="%s_bank%d" % (name, b), tag="bank")
+                for u in range(2):
+                    for a2 in range(2):
+                        start = (2 * b + a2) * 2 * P
+                        nc.tensor.transpose(
+                            bank[:, (2 * u + a2) * P : (2 * u + a2 + 1) * P],
+                            words[:, start + u : start + 2 * P : 2],
+                            ident[:],
+                        )
+                nc.scalar.copy(
+                    out=grouped_words[:, b * half : (b + 1) * half].rearrange(
+                        "p (n u) -> p n u", u=2
+                    ),
+                    in_=bank[:].rearrange("p (u n) -> p n u", u=2),
+                )
+            return grouped
+
+        def negate(grouped, name):
+            minus = grouped_pool.tile(
+                [P, SIZE * PACK], BF16, name=name, tag="grouped", align_bytes=64
+            )
+            nc.vector.tensor_scalar_mul(out=minus[:], in0=grouped[:], scalar1=-1.0)
+            return minus
+
+        def quantise(grouped, name):
+            codes = mx_pool.tile([P, SIZE], U32, name=name + "_codes", align_bytes=64)
+            scales = mx_pool.tile([P, SIZE], U8, name=name + "_scales", align_bytes=64)
+            nc.vector.quantize_mx(out=codes[:].bitcast(FP8X4), scales=scales[:], in_=grouped[:])
+            return codes, scales
+
+        def mx_pass(acc, stationary, tile_index, moving, c):
+            s_codes, s_scales = stationary
+            m_codes, m_scales = moving
+            cols = slice(tile_index * P, (tile_index + 1) * P)
+            nc.tensor.matmul_mx(
+                out=acc[:],
+                lhsT=s_codes[:, cols].bitcast(FP8X4),
+                lhsT_scale=s_scales[:, cols],
+                rhs=m_codes[:].bitcast(FP8X4),
+                rhs_scale=m_scales[:],
+                start=(c == 0),
+                stop=(c == PARTS - 1),
+            )
+
+        q_mx = {}
+        w1_mx = {}
+        w2_mx = {}
+        h_mx = {}
+
+        def layer1_pass(acc, o, t, c):
+            mx_pass(acc, w1_mx[HAMILTON[o][c]], t, q_mx[c], c)
+
+        def layer2_pass(acc, a, o, c):
+            mx_pass(acc, h_mx[c], a, w2_mx[HAMILTON[o][c]], c)
+
+        def hidden_out_of_psum(acc, planar, o, t):
+            nc.scalar.activation(
+                out=planar[:, t, :],
+                in_=acc[:],
+                func=mybir.ActivationFunctionType.Relu,
+                bias=b1_sb[:, o, t : t + 1],
+                scale=1.0,
+            )
+
+        def quantise_hidden(planar, o):
+            grouped = grouped_pool.tile(
+                [P, SIZE * PACK], BF16, name="h_grouped%d" % o, tag="grouped", align_bytes=64
+            )
+            nc.vector.tensor_copy(
+                out=grouped[:].rearrange("p (n i t) -> p n t i", i=4, t=PACK),
+                in_=planar[:].rearrange("p t (n i) -> p n t i", i=4),
+            )
+            h_mx[o] = quantise(grouped, "h%d" % o)
+
+        def transpose_w2(w):
+            return transpose_component(w2_raw[w], "w2_grouped%d" % w)
+
+        def quantise_w2(w, grouped):
+            if w > 0:
+                w2_mx[(w, -1)] = quantise(negate(grouped, "w2_minus%d" % w), "w2_minus%d" % w)
+            w2_mx[(w, 1)] = quantise(grouped, "w2_plus%d" % w)
+
+        def store_output(acc, a, o):
+            result = result_pool.tile([P, SIZE], F32, name="result", tag="result")
+            nc.vector.tensor_tensor(
+                out=result[:], in0=acc[:], in1=b2_sb[:, o, :], op=mybir.AluOpType.add
+            )
+            nc.sync.dma_start(
+                out=outs[o].rearrange("(p a) n -> p a n", a=TILES)[:, a, :], in_=result[:]
+            )
+
+        def transpose_pair(c):
+            w1_grouped[c] = transpose_component(w1_raw[c], "w1_grouped%d" % c)
+            q_grouped[c] = transpose_component(q_raw[c], "q_grouped%d" % c)
+
+        q_grouped = {}
+        w1_grouped = {}
+        w2_grouped = {}
+        transpose_pair(0)
+        acc_r = [psum.tile([P, SIZE], F32, name="acc_r%d" % t, tag="bank") for t in range(TILES)]
+        for c in range(PARTS):
+            if c + 1 < PARTS:
+                transpose_pair(c + 1)
+            else:
+                w2_grouped[0] = transpose_w2(0)
+                w2_grouped[1] = transpose_w2(1)
+            if c > 0:
+                minus = negate(w1_grouped[c], "w1_minus%d" % c)
+            q_mx[c] = quantise(q_grouped[c], "q%d" % c)
+            if c > 0:
+                w1_mx[(c, -1)] = quantise(minus, "w1_minus%d" % c)
+            w1_mx[(c, 1)] = quantise(w1_grouped[c], "w1_plus%d" % c)
+            for t in range(TILES):
+                layer1_pass(acc_r[t], 0, t, c)
+        quantise_w2(0, w2_grouped[0])
+        quantise_w2(1, w2_grouped[1])
+        planar = planar_pool.tile([P, TILES, SIZE], BF16, name="planar", tag="planar")
+        for t in range(TILES):
+            hidden_out_of_psum(acc_r[t], planar, 0, t)
+        quantise_hidden(planar, 0)
+
+        def layer1_component(o):
+            planar = planar_pool.tile([P, TILES, SIZE], BF16, name="planar", tag="planar")
+            for t in range(TILES):
+                acc = psum.tile([P, SIZE], F32, name="acc1", tag="bank")
+                for c in range(PARTS):
+                    layer1_pass(acc, o, t, c)
+                hidden_out_of_psum(acc, planar, o, t)
+            quantise_hidden(planar, o)
+
+        layer1_component(1)
+        w2_grouped[2] = transpose_w2(2)
+        w2_grouped[3] = transpose_w2(3)
+        quantise_w2(2, w2_grouped[2])
+        quantise_w2(3, w2_grouped[3])
+        layer1_component(2)
+        layer1_component(3)
+
+        acc_0 = [psum.tile([P, SIZE], F32, name="acc_0%d" % o, tag="bank") for o in range(PARTS)]
+        for c in range(PARTS):
+            for o in range(PARTS):
+                layer2_pass(acc_0[o], 0, o, c)
+        for o in range(PARTS):
+            store_output(acc_0[o], 0, o)
+        for a in range(1, TILES):
+            for o in range(PARTS):
+                acc = psum.tile([P, SIZE], F32, name="acc2", tag="bank")
+                for c in range(PARTS):
+                    layer2_pass(acc, a, o, c)
+                store_output(acc, a, o)

@@ -14,15 +14,20 @@ SIZE = 512
 TILES = SIZE // P
 PACK = 4
 PARTS = 4
+HALF = SIZE // 2
+BLOCK = 32
 
 FLOPS = 2 * 2 * SIZE * (PARTS * SIZE) * (PARTS * SIZE)
 
-HAMILTON = (
-    ((0, 1), (1, -1), (2, -1), (3, -1)),
+SIGNED = (
+    ((0, -1), (1, 1), (2, 1), (3, 1)),
     ((1, 1), (0, 1), (3, 1), (2, -1)),
     ((2, 1), (3, -1), (0, 1), (1, 1)),
-    ((3, 1), (2, 1), (1, -1), (0, 1)),
+    ((3, -1), (2, -1), (1, 1), (0, -1)),
 )
+FLIP = (-1, 1, 1, -1)
+
+ALL_COLS = slice(0, SIZE)
 
 
 def tile_qmlp_kernel(
@@ -45,10 +50,11 @@ def tile_qmlp_kernel(
     with ExitStack() as ctx:
         const = ctx.enter_context(tc.tile_pool(name="const", bufs=1))
         raw_pool = ctx.enter_context(tc.tile_pool(name="raw", bufs=1))
-        grouped_pool = ctx.enter_context(tc.tile_pool(name="grouped", bufs=8))
-        planar_pool = ctx.enter_context(tc.tile_pool(name="planar", bufs=2))
+        grouped_pool = ctx.enter_context(tc.tile_pool(name="grouped", bufs=10))
+        planar_pool = ctx.enter_context(tc.tile_pool(name="planar", bufs=4))
+        w2_pool = ctx.enter_context(tc.tile_pool(name="w2", bufs=2))
         mx_pool = ctx.enter_context(tc.tile_pool(name="mx", bufs=1))
-        result_pool = ctx.enter_context(tc.tile_pool(name="result", bufs=4))
+        result_pool = ctx.enter_context(tc.tile_pool(name="result", bufs=8))
         psum = ctx.enter_context(tc.psum_pool(name="psum", bufs=8))
         ctx.enter_context(tc.manual_schedule())
 
@@ -57,20 +63,28 @@ def tile_qmlp_kernel(
             nc.sync.dma_start(out=raw[:].rearrange("p (n x) -> p n x", n=view.shape[1]), in_=view)
             return raw
 
-        q_raw = []
-        w1_raw = []
-        for c in range(PARTS):
-            w1_raw.append(load("w1_raw%d" % c, w1[c].rearrange("(p t) k -> p t k", t=TILES)))
-            q_raw.append(load("q_raw%d" % c, q[c].rearrange("(p a) k -> p a k", a=TILES)))
+        q_raw = {}
+        w1_raw = {}
+        for c in (1, 2, 3, 0):
+            w1_raw[c] = load("w1_raw%d" % c, w1[c].rearrange("(p t) k -> p t k", t=TILES))
+            q_raw[c] = load("q_raw%d" % c, q[c].rearrange("(p a) k -> p a k", a=TILES))
         b1_sb = const.tile([P, PARTS, 16], BF16, name="b1_sb")
         for c in range(PARTS):
             nc.sync.dma_start(
                 out=b1_sb[:, c, 0:TILES],
                 in_=b1[c].rearrange("(p t) -> p t", t=TILES),
             )
-        w2_raw = [
-            load("w2_raw%d" % c, w2[c].rearrange("(a p) k -> p a k", p=P)) for c in range(PARTS)
-        ]
+        w2_raw = {}
+        for c in (0, 1):
+            w2_raw[c] = load("w2_raw%d" % c, w2[c].rearrange("(a p) k -> p a k", p=P))
+        for c in (3, 2):
+            raw = raw_pool.tile([P, TILES * SIZE], BF16, name="w2_raw%d" % c)
+            for Q in range(P // BLOCK):
+                nc.sync.dma_start(
+                    out=raw[Q * BLOCK : (Q + 1) * BLOCK, :].rearrange("j (b k) -> j b k", k=P),
+                    in_=w2[c].rearrange("(b j) k -> j b k", j=BLOCK)[:, :, Q * P : (Q + 1) * P],
+                )
+            w2_raw[c] = raw
         b2_sb = const.tile([P, PARTS, SIZE], BF16, name="b2_sb")
         for c in range(PARTS):
             nc.sync.dma_start(out=b2_sb[:, c, :], in_=b2[c].partition_broadcast(P))
@@ -78,11 +92,14 @@ def tile_qmlp_kernel(
         ident = const.tile([P, P], F32, name="ident")
         make_identity(nc, ident[:])
 
-        def transpose_component(raw, name):
-            words = raw[:].bitcast(F32)
-            grouped = grouped_pool.tile(
+        def grouped_tile(name):
+            return grouped_pool.tile(
                 [P, SIZE * PACK], BF16, name=name, tag="grouped", align_bytes=64
             )
+
+        def transpose_component(raw, name):
+            words = raw[:].bitcast(F32)
+            grouped = grouped_tile(name)
             grouped_words = grouped[:].bitcast(F32)
             half = SIZE
             for b in range(2):
@@ -104,30 +121,38 @@ def tile_qmlp_kernel(
             return grouped
 
         def negate(grouped, name):
-            minus = grouped_pool.tile(
-                [P, SIZE * PACK], BF16, name=name, tag="grouped", align_bytes=64
-            )
+            minus = grouped_tile(name)
             nc.vector.tensor_scalar_mul(out=minus[:], in0=grouped[:], scalar1=-1.0)
             return minus
 
-        def quantise(grouped, name):
+        def mx_operand(name):
             codes = mx_pool.tile([P, SIZE], U32, name=name + "_codes", align_bytes=64)
             scales = mx_pool.tile([P, SIZE], U8, name=name + "_scales", align_bytes=64)
-            nc.vector.quantize_mx(out=codes[:].bitcast(FP8X4), scales=scales[:], in_=grouped[:])
             return codes, scales
 
-        def mx_pass(acc, stationary, tile_index, moving, c):
+        def quantise_into(operand, cols, values):
+            codes, scales = operand
+            nc.vector.quantize_mx(
+                out=codes[:, cols].bitcast(FP8X4), scales=scales[:, cols], in_=values
+            )
+
+        def quantise(grouped, name):
+            operand = mx_operand(name)
+            quantise_into(operand, ALL_COLS, grouped[:])
+            return operand
+
+        def mx_pass(acc, stationary, tile_index, moving, moving_cols, start, stop):
             s_codes, s_scales = stationary
             m_codes, m_scales = moving
             cols = slice(tile_index * P, (tile_index + 1) * P)
             nc.tensor.matmul_mx(
-                out=acc[:],
+                out=acc,
                 lhsT=s_codes[:, cols].bitcast(FP8X4),
                 lhsT_scale=s_scales[:, cols],
-                rhs=m_codes[:].bitcast(FP8X4),
-                rhs_scale=m_scales[:],
-                start=(c == 0),
-                stop=(c == PARTS - 1),
+                rhs=m_codes[:, moving_cols].bitcast(FP8X4),
+                rhs_scale=m_scales[:, moving_cols],
+                start=start,
+                stop=stop,
             )
 
         q_mx = {}
@@ -135,104 +160,178 @@ def tile_qmlp_kernel(
         w2_mx = {}
         h_mx = {}
 
-        def layer1_pass(acc, o, t, c):
-            mx_pass(acc, w1_mx[HAMILTON[o][c]], t, q_mx[c], c)
+        def four_banks(name):
+            return [psum.tile([P, SIZE], F32, name="%s%d" % (name, t), tag="bank") for t in range(TILES)]
 
-        def layer2_pass(acc, a, o, c):
-            mx_pass(acc, h_mx[c], a, w2_mx[HAMILTON[o][c]], c)
+        def layer1_pass(acc, o, t, c, rows, start, stop):
+            mx_pass(acc, w1_mx[SIGNED[o][c]], t, q_mx[c], rows, start, stop)
+
+        def layer1_term(acc, o, c, start=False, stop=False):
+            for t in range(TILES):
+                layer1_pass(acc[t][:], o, t, c, ALL_COLS, start, stop)
+
+        def layer2_pass(acc, a, o, c, start, stop):
+            mx_pass(acc[:], h_mx[c], a, w2_mx[SIGNED[o][c]], ALL_COLS, start, stop)
 
         def hidden_out_of_psum(acc, planar, o, t):
             nc.scalar.activation(
-                out=planar[:, t, :],
-                in_=acc[:],
+                out=planar,
+                in_=acc,
                 func=mybir.ActivationFunctionType.Relu,
                 bias=b1_sb[:, o, t : t + 1],
-                scale=1.0,
+                scale=float(FLIP[o]),
             )
 
-        def quantise_hidden(planar, o):
-            grouped = grouped_pool.tile(
-                [P, SIZE * PACK], BF16, name="h_grouped%d" % o, tag="grouped", align_bytes=64
-            )
+        def hidden_tile():
+            return planar_pool.tile([P, TILES, SIZE], BF16, name="planar", tag="planar")
+
+        def quantise_hidden(planar, o, rows):
+            grouped = grouped_tile("h_grouped%d" % o)
+            count = rows.stop - rows.start
             nc.vector.tensor_copy(
-                out=grouped[:].rearrange("p (n i t) -> p n t i", i=4, t=PACK),
-                in_=planar[:].rearrange("p t (n i) -> p n t i", i=4),
+                out=grouped[:, 0 : count * PACK].rearrange("p (n i t) -> p n t i", i=4, t=PACK),
+                in_=planar[:, :, rows].rearrange("p t (n i) -> p n t i", i=4),
             )
-            h_mx[o] = quantise(grouped, "h%d" % o)
-
-        def transpose_w2(w):
-            return transpose_component(w2_raw[w], "w2_grouped%d" % w)
-
-        def quantise_w2(w, grouped):
-            if w > 0:
-                w2_mx[(w, -1)] = quantise(negate(grouped, "w2_minus%d" % w), "w2_minus%d" % w)
-            w2_mx[(w, 1)] = quantise(grouped, "w2_plus%d" % w)
+            if o not in h_mx:
+                h_mx[o] = mx_operand("h%d" % o)
+            quantise_into(h_mx[o], rows, grouped[:, 0 : count * PACK])
 
         def store_output(acc, a, o):
             result = result_pool.tile([P, SIZE], F32, name="result", tag="result")
-            nc.vector.tensor_tensor(
-                out=result[:], in0=acc[:], in1=b2_sb[:, o, :], op=mybir.AluOpType.add
-            )
+            if FLIP[o] > 0:
+                nc.vector.tensor_tensor(
+                    out=result[:], in0=acc[:], in1=b2_sb[:, o, :], op=mybir.AluOpType.add
+                )
+            else:
+                nc.vector.tensor_tensor(
+                    out=result[:], in0=b2_sb[:, o, :], in1=acc[:], op=mybir.AluOpType.subtract
+                )
             nc.sync.dma_start(
                 out=outs[o].rearrange("(p a) n -> p a n", a=TILES)[:, a, :], in_=result[:]
             )
+
+        q_grouped = {}
+        w1_grouped = {}
+        w2_split = {}
+        w2_turned = {}
+        w2_grouped = {}
 
         def transpose_pair(c):
             w1_grouped[c] = transpose_component(w1_raw[c], "w1_grouped%d" % c)
             q_grouped[c] = transpose_component(q_raw[c], "q_grouped%d" % c)
 
-        q_grouped = {}
-        w1_grouped = {}
-        w2_grouped = {}
-        transpose_pair(0)
-        acc_r = [psum.tile([P, SIZE], F32, name="acc_r%d" % t, tag="bank") for t in range(TILES)]
-        for c in range(PARTS):
-            if c + 1 < PARTS:
-                transpose_pair(c + 1)
-            else:
-                w2_grouped[0] = transpose_w2(0)
-                w2_grouped[1] = transpose_w2(1)
-            if c > 0:
-                minus = negate(w1_grouped[c], "w1_minus%d" % c)
+        def transpose_w2(w):
+            w2_grouped[w] = transpose_component(w2_raw[w], "w2_grouped%d" % w)
+
+        def split_w2(w):
+            split = w2_pool.tile([P, TILES * SIZE], BF16, name="split", align_bytes=64)
+            nc.scalar.copy(
+                out=split[:].bitcast(F32).rearrange("p (v m) -> p v m", v=2),
+                in_=w2_raw[w][:].bitcast(F32).rearrange("p (m v) -> p v m", v=2),
+            )
+            w2_split[w] = split
+
+        def turn_w2(w):
+            turned = w2_pool.tile([P, TILES * SIZE], BF16, name="turned", align_bytes=64)
+            nc.vector.transpose(out=turned[:].bitcast(F32), in_=w2_split[w][:].bitcast(F32))
+            w2_turned[w] = turned
+
+        def group_w2(w):
+            grouped = grouped_tile("w2_grouped%d" % w)
+            nc.scalar.copy(
+                out=grouped[:].bitcast(F32).rearrange("p (n v) -> p n v", v=2),
+                in_=w2_turned[w][:].bitcast(F32).rearrange("p (v n) -> p n v", v=2),
+            )
+            w2_grouped[w] = grouped
+
+        def quantise_q(c):
             q_mx[c] = quantise(q_grouped[c], "q%d" % c)
-            if c > 0:
-                w1_mx[(c, -1)] = quantise(minus, "w1_minus%d" % c)
-            w1_mx[(c, 1)] = quantise(w1_grouped[c], "w1_plus%d" % c)
-            for t in range(TILES):
-                layer1_pass(acc_r[t], 0, t, c)
-        quantise_w2(0, w2_grouped[0])
-        quantise_w2(1, w2_grouped[1])
-        planar = planar_pool.tile([P, TILES, SIZE], BF16, name="planar", tag="planar")
+
+        def quantise_w1(w, sign):
+            if sign < 0:
+                w1_mx[(w, -1)] = quantise(negate(w1_grouped[w], "w1_neg%d" % w), "w1_minus%d" % w)
+            else:
+                w1_mx[(w, 1)] = quantise(w1_grouped[w], "w1_plus%d" % w)
+
+        def quantise_w2(w, sign):
+            if sign < 0:
+                w2_mx[(w, -1)] = quantise(negate(w2_grouped[w], "w2_neg%d" % w), "w2_minus%d" % w)
+            else:
+                w2_mx[(w, 1)] = quantise(w2_grouped[w], "w2_plus%d" % w)
+
+        transpose_pair(1)
+        transpose_pair(2)
+        quantise_q(1)
+        quantise_w1(1, 1)
+        acc0 = four_banks("acc0")
+        transpose_pair(3)
+        quantise_q(2)
+        quantise_w1(2, 1)
+        layer1_term(acc0, 0, 1, start=True)
+        transpose_pair(0)
+        quantise_w1(2, -1)
+        quantise_q(3)
+        quantise_w1(3, 1)
+        layer1_term(acc0, 0, 2)
+        layer1_term(acc0, 0, 3)
+        transpose_w2(0)
+        transpose_w2(1)
+        quantise_q(0)
+        quantise_w1(0, -1)
+        layer1_term(acc0, 0, 0, stop=True)
+        quantise_w1(0, 1)
+        quantise_w1(3, -1)
+        planar0 = hidden_tile()
         for t in range(TILES):
-            hidden_out_of_psum(acc_r[t], planar, 0, t)
-        quantise_hidden(planar, 0)
+            hidden_out_of_psum(acc0[t][:], planar0[:, t, :], 0, t)
+        quantise_w2(0, 1)
+        quantise_w2(1, 1)
 
-        def layer1_component(o):
-            planar = planar_pool.tile([P, TILES, SIZE], BF16, name="planar", tag="planar")
+        split_w2(3)
+        planar1 = hidden_tile()
+        for t in range(TILES):
+            acc = psum.tile([P, SIZE], F32, name="acc1", tag="bank")
+            for c in range(PARTS):
+                layer1_pass(acc[:], 1, t, c, ALL_COLS, c == 0, c == PARTS - 1)
+            hidden_out_of_psum(acc[:], planar1[:, t, :], 1, t)
+        quantise_hidden(planar0, 0, ALL_COLS)
+        turn_w2(3)
+        split_w2(2)
+        quantise_hidden(planar1, 1, ALL_COLS)
+
+        planar2 = hidden_tile()
+        planar3 = hidden_tile()
+
+        def layer1_half(o, planar, half):
+            rows = slice(half * HALF, (half + 1) * HALF)
             for t in range(TILES):
-                acc = psum.tile([P, SIZE], F32, name="acc1", tag="bank")
+                acc = psum.tile([P, HALF], F32, name="acc_half", tag="bank")
                 for c in range(PARTS):
-                    layer1_pass(acc, o, t, c)
-                hidden_out_of_psum(acc, planar, o, t)
-            quantise_hidden(planar, o)
+                    layer1_pass(acc[:], o, t, c, rows, c == 0, c == PARTS - 1)
+                hidden_out_of_psum(acc[:], planar[:, t, rows], o, t)
+            return rows
 
-        layer1_component(1)
-        w2_grouped[2] = transpose_w2(2)
-        w2_grouped[3] = transpose_w2(3)
-        quantise_w2(2, w2_grouped[2])
-        quantise_w2(3, w2_grouped[3])
-        layer1_component(2)
-        layer1_component(3)
+        rows = layer1_half(2, planar2, 0)
+        turn_w2(2)
+        group_w2(3)
+        quantise_hidden(planar2, 2, rows)
+        rows = layer1_half(3, planar3, 0)
+        quantise_w2(3, 1)
+        group_w2(2)
+        quantise_hidden(planar3, 3, rows)
+        quantise_w2(2, -1)
+        rows = layer1_half(2, planar2, 1)
+        quantise_w2(2, 1)
+        quantise_w2(3, -1)
+        quantise_hidden(planar2, 2, rows)
+        rows = layer1_half(3, planar3, 1)
+        quantise_w2(0, -1)
+        quantise_hidden(planar3, 3, rows)
 
-        acc_0 = [psum.tile([P, SIZE], F32, name="acc_0%d" % o, tag="bank") for o in range(PARTS)]
-        for c in range(PARTS):
-            for o in range(PARTS):
-                layer2_pass(acc_0[o], 0, o, c)
-        for o in range(PARTS):
-            store_output(acc_0[o], 0, o)
-        for a in range(1, TILES):
-            for o in range(PARTS):
-                acc = psum.tile([P, SIZE], F32, name="acc2", tag="bank")
-                for c in range(PARTS):
-                    layer2_pass(acc, a, o, c)
-                store_output(acc, a, o)
+        for half in range(2):
+            for o in (1, 2, 0, 3):
+                for a in (2 * half, 2 * half + 1):
+                    acc = psum.tile([P, SIZE], F32, name="acc2", tag="bank")
+                    for c in range(PARTS):
+                        layer2_pass(acc, a, o, c, c == 0, c == PARTS - 1)
+                    store_output(acc, a, o)

@@ -58,33 +58,38 @@ def tile_qmlp_kernel(
         psum = ctx.enter_context(tc.psum_pool(name="psum", bufs=8))
         ctx.enter_context(tc.manual_schedule())
 
-        def load(name, view):
+        def load(name, view, pieces=1):
             raw = raw_pool.tile([P, TILES * SIZE], BF16, name=name)
-            nc.sync.dma_start(out=raw[:].rearrange("p (n x) -> p n x", n=view.shape[1]), in_=view)
+            tiles = TILES // pieces
+            for n in range(0, TILES, tiles):
+                nc.sync.dma_start(
+                    out=raw[:].rearrange("p (n x) -> p n x", n=TILES)[:, n : n + tiles, :],
+                    in_=view[:, n : n + tiles, :],
+                )
             return raw
 
         q_raw = {}
         w1_raw = {}
         for c in (1, 2, 3, 0):
-            w1_raw[c] = load("w1_raw%d" % c, w1[c].rearrange("(p t) k -> p t k", t=TILES))
-            q_raw[c] = load("q_raw%d" % c, q[c].rearrange("(p a) k -> p a k", a=TILES))
+            pieces = 2 if c == 1 else 1
+            w1_raw[c] = load("w1_raw%d" % c, w1[c].rearrange("(p t) k -> p t k", t=TILES), pieces)
+            q_raw[c] = load("q_raw%d" % c, q[c].rearrange("(p a) k -> p a k", a=TILES), pieces)
         b1_sb = const.tile([P, PARTS, 16], BF16, name="b1_sb")
         for c in range(PARTS):
             nc.sync.dma_start(
                 out=b1_sb[:, c, 0:TILES],
                 in_=b1[c].rearrange("(p t) -> p t", t=TILES),
             )
-        w2_raw = {}
-        for c in (0, 1):
-            w2_raw[c] = load("w2_raw%d" % c, w2[c].rearrange("(a p) k -> p a k", p=P))
-        for c in (3, 2):
+        def load_w2_blocks(c):
             raw = raw_pool.tile([P, TILES * SIZE], BF16, name="w2_raw%d" % c)
             for Q in range(P // BLOCK):
                 nc.sync.dma_start(
                     out=raw[Q * BLOCK : (Q + 1) * BLOCK, :].rearrange("j (b k) -> j b k", k=P),
                     in_=w2[c].rearrange("(b j) k -> j b k", j=BLOCK)[:, :, Q * P : (Q + 1) * P],
                 )
-            w2_raw[c] = raw
+            return raw
+
+        w2_raw = {w: load_w2_blocks(w) for w in (1, 0, 3, 2)}
         b2_sb = const.tile([P, PARTS, SIZE], BF16, name="b2_sb")
         for c in range(PARTS):
             nc.sync.dma_start(out=b2_sb[:, c, :], in_=b2[c].partition_broadcast(P))
@@ -220,12 +225,9 @@ def tile_qmlp_kernel(
             w1_grouped[c] = transpose_component(w1_raw[c], "w1_grouped%d" % c)
             q_grouped[c] = transpose_component(q_raw[c], "q_grouped%d" % c)
 
-        def transpose_w2(w):
-            w2_grouped[w] = transpose_component(w2_raw[w], "w2_grouped%d" % w)
-
-        def split_w2(w):
+        def split_w2(w, copy):
             split = w2_pool.tile([P, TILES * SIZE], BF16, name="split", align_bytes=64)
-            nc.scalar.copy(
+            copy(
                 out=split[:].bitcast(F32).rearrange("p (v m) -> p v m", v=2),
                 in_=w2_raw[w][:].bitcast(F32).rearrange("p (m v) -> p v m", v=2),
             )
@@ -236,9 +238,9 @@ def tile_qmlp_kernel(
             nc.vector.transpose(out=turned[:].bitcast(F32), in_=w2_split[w][:].bitcast(F32))
             w2_turned[w] = turned
 
-        def group_w2(w):
+        def group_w2(w, copy):
             grouped = grouped_tile("w2_grouped%d" % w)
-            nc.scalar.copy(
+            copy(
                 out=grouped[:].bitcast(F32).rearrange("p (n v) -> p n v", v=2),
                 in_=w2_turned[w][:].bitcast(F32).rearrange("p (v n) -> p n v", v=2),
             )
@@ -261,72 +263,77 @@ def tile_qmlp_kernel(
 
         transpose_pair(1)
         transpose_pair(2)
-        quantise_q(1)
         quantise_w1(1, 1)
-        acc0 = four_banks("acc0")
+        quantise_q(1)
         transpose_pair(3)
-        quantise_q(2)
         quantise_w1(2, 1)
-        layer1_term(acc0, 0, 1, start=True)
-        transpose_pair(0)
         quantise_w1(2, -1)
-        quantise_q(3)
+        quantise_q(2)
+        transpose_pair(0)
         quantise_w1(3, 1)
+        quantise_w1(3, -1)
+        quantise_q(3)
+        acc0 = four_banks("acc0")
+        layer1_term(acc0, 0, 1, start=True)
         layer1_term(acc0, 0, 2)
         layer1_term(acc0, 0, 3)
-        transpose_w2(0)
-        transpose_w2(1)
-        quantise_q(0)
         quantise_w1(0, -1)
+        quantise_q(0)
         layer1_term(acc0, 0, 0, stop=True)
         quantise_w1(0, 1)
-        quantise_w1(3, -1)
+        split_w2(1, nc.scalar.copy)
+        turn_w2(1)
+        group_w2(1, nc.vector.tensor_copy)
+        quantise_w2(1, 1)
+        split_w2(0, nc.scalar.copy)
+        turn_w2(0)
         planar0 = hidden_tile()
         for t in range(TILES):
             hidden_out_of_psum(acc0[t][:], planar0[:, t, :], 0, t)
-        quantise_w2(0, 1)
-        quantise_w2(1, 1)
 
-        split_w2(3)
         planar1 = hidden_tile()
         for t in range(TILES):
             acc = psum.tile([P, SIZE], F32, name="acc1", tag="bank")
             for c in range(PARTS):
                 layer1_pass(acc[:], 1, t, c, ALL_COLS, c == 0, c == PARTS - 1)
             hidden_out_of_psum(acc[:], planar1[:, t, :], 1, t)
+            if t == 0:
+                split_w2(3, nc.scalar.copy)
+            if t == 1:
+                group_w2(0, nc.scalar.copy)
         quantise_hidden(planar0, 0, ALL_COLS)
         turn_w2(3)
-        split_w2(2)
+        quantise_w2(0, 1)
         quantise_hidden(planar1, 1, ALL_COLS)
 
         planar2 = hidden_tile()
         planar3 = hidden_tile()
 
-        def layer1_half(o, planar, half):
-            rows = slice(half * HALF, (half + 1) * HALF)
+        def layer1_half(o, planar, rows, scalar_step=None):
             for t in range(TILES):
                 acc = psum.tile([P, HALF], F32, name="acc_half", tag="bank")
                 for c in range(PARTS):
                     layer1_pass(acc[:], o, t, c, rows, c == 0, c == PARTS - 1)
                 hidden_out_of_psum(acc[:], planar[:, t, rows], o, t)
-            return rows
+                if t == 1 and scalar_step:
+                    scalar_step()
 
-        rows = layer1_half(2, planar2, 0)
+        first, second = slice(0, HALF), slice(HALF, SIZE)
+        layer1_half(2, planar2, first, lambda: split_w2(2, nc.scalar.copy))
+        quantise_hidden(planar2, 2, first)
         turn_w2(2)
-        group_w2(3)
-        quantise_hidden(planar2, 2, rows)
-        rows = layer1_half(3, planar3, 0)
+        layer1_half(3, planar3, first, lambda: group_w2(3, nc.scalar.copy))
+        quantise_hidden(planar3, 3, first)
+        group_w2(2, nc.scalar.copy)
         quantise_w2(3, 1)
-        group_w2(2)
-        quantise_hidden(planar3, 3, rows)
         quantise_w2(2, -1)
-        rows = layer1_half(2, planar2, 1)
         quantise_w2(2, 1)
         quantise_w2(3, -1)
-        quantise_hidden(planar2, 2, rows)
-        rows = layer1_half(3, planar3, 1)
+        layer1_half(2, planar2, second)
+        layer1_half(3, planar3, second)
         quantise_w2(0, -1)
-        quantise_hidden(planar3, 3, rows)
+        quantise_hidden(planar2, 2, second)
+        quantise_hidden(planar3, 3, second)
 
         for half in range(2):
             for o in (1, 2, 0, 3):

@@ -71,7 +71,7 @@ def tile_qmlp_kernel(
         q_raw = {}
         w1_raw = {}
         for c in (1, 2, 3, 0):
-            pieces = 2 if c == 1 else 1
+            pieces = 2 if c in (1, 0) else 1
             w1_raw[c] = load("w1_raw%d" % c, w1[c].rearrange("(p t) k -> p t k", t=TILES), pieces)
             q_raw[c] = load("q_raw%d" % c, q[c].rearrange("(p a) k -> p a k", a=TILES), pieces)
         b1_sb = const.tile([P, PARTS, 16], BF16, name="b1_sb")
@@ -80,6 +80,8 @@ def tile_qmlp_kernel(
                 out=b1_sb[:, c, 0:TILES],
                 in_=b1[c].rearrange("(p t) -> p t", t=TILES),
             )
+        w2_raw = {w: load("w2_raw%d" % w, w2[w].rearrange("(a p) k -> p a k", p=P)) for w in (1, 0)}
+
         def load_w2_blocks(c):
             raw = raw_pool.tile([P, TILES * SIZE], BF16, name="w2_raw%d" % c)
             for Q in range(P // BLOCK):
@@ -89,7 +91,8 @@ def tile_qmlp_kernel(
                 )
             return raw
 
-        w2_raw = {w: load_w2_blocks(w) for w in (1, 0, 3, 2)}
+        for w in (3, 2):
+            w2_raw[w] = load_w2_blocks(w)
         b2_sb = const.tile([P, PARTS, SIZE], BF16, name="b2_sb")
         for c in range(PARTS):
             nc.sync.dma_start(out=b2_sb[:, c, :], in_=b2[c].partition_broadcast(P))
@@ -175,8 +178,8 @@ def tile_qmlp_kernel(
             for t in range(TILES):
                 layer1_pass(acc[t][:], o, t, c, ALL_COLS, start, stop)
 
-        def layer2_pass(acc, a, o, c, start, stop):
-            mx_pass(acc[:], h_mx[c], a, w2_mx[SIGNED[o][c]], ALL_COLS, start, stop)
+        def layer2_pass(acc, a, o, c, features, start, stop):
+            mx_pass(acc, h_mx[c], a, w2_mx[SIGNED[o][c]], features, start, stop)
 
         def hidden_out_of_psum(acc, planar, o, t):
             nc.scalar.activation(
@@ -201,18 +204,23 @@ def tile_qmlp_kernel(
                 h_mx[o] = mx_operand("h%d" % o)
             quantise_into(h_mx[o], rows, grouped[:, 0 : count * PACK])
 
-        def store_output(acc, a, o):
-            result = result_pool.tile([P, SIZE], F32, name="result", tag="result")
+        def output_tile(a, o, features):
+            width = features.stop - features.start
+            acc = psum.tile([P, width], F32, name="acc2", tag="bank")
+            for c in range(PARTS):
+                layer2_pass(acc[:], a, o, c, features, c == 0, c == PARTS - 1)
+            result = result_pool.tile([P, width], F32, name="result", tag="result")
+            bias = b2_sb[:, o, features]
             if FLIP[o] > 0:
                 nc.vector.tensor_tensor(
-                    out=result[:], in0=acc[:], in1=b2_sb[:, o, :], op=mybir.AluOpType.add
+                    out=result[:], in0=acc[:], in1=bias, op=mybir.AluOpType.add
                 )
             else:
                 nc.vector.tensor_tensor(
-                    out=result[:], in0=b2_sb[:, o, :], in1=acc[:], op=mybir.AluOpType.subtract
+                    out=result[:], in0=bias, in1=acc[:], op=mybir.AluOpType.subtract
                 )
             nc.sync.dma_start(
-                out=outs[o].rearrange("(p a) n -> p a n", a=TILES)[:, a, :], in_=result[:]
+                out=outs[o].rearrange("(p a) n -> p a n", a=TILES)[:, a, features], in_=result[:]
             )
 
         q_grouped = {}
@@ -224,6 +232,28 @@ def tile_qmlp_kernel(
         def transpose_pair(c):
             w1_grouped[c] = transpose_component(w1_raw[c], "w1_grouped%d" % c)
             q_grouped[c] = transpose_component(q_raw[c], "q_grouped%d" % c)
+
+        def transpose_w2(w):
+            words = w2_split[w][:].bitcast(F32)
+            grouped = grouped_tile("w2_grouped%d" % w)
+            grouped_words = grouped[:].bitcast(F32)
+            for b in range(2):
+                bank = psum.tile([P, SIZE], F32, name="w2_bank", tag="bank")
+                for u in range(2):
+                    for a2 in range(2):
+                        start = u * SIZE + (2 * b + a2) * P
+                        nc.tensor.transpose(
+                            bank[:, (2 * u + a2) * P : (2 * u + a2 + 1) * P],
+                            words[:, start : start + P],
+                            ident[:],
+                        )
+                nc.scalar.copy(
+                    out=grouped_words[:, b * SIZE : (b + 1) * SIZE].rearrange(
+                        "p (n u) -> p n u", u=2
+                    ),
+                    in_=bank[:].rearrange("p (u n) -> p n u", u=2),
+                )
+            w2_grouped[w] = grouped
 
         def split_w2(w, copy):
             split = w2_pool.tile([P, TILES * SIZE], BF16, name="split", align_bytes=64)
@@ -277,19 +307,19 @@ def tile_qmlp_kernel(
         layer1_term(acc0, 0, 1, start=True)
         layer1_term(acc0, 0, 2)
         layer1_term(acc0, 0, 3)
+        split_w2(1, nc.scalar.copy)
+        split_w2(0, nc.scalar.copy)
+        transpose_w2(1)
         quantise_w1(0, -1)
         quantise_q(0)
         layer1_term(acc0, 0, 0, stop=True)
+        transpose_w2(0)
         quantise_w1(0, 1)
-        split_w2(1, nc.scalar.copy)
-        turn_w2(1)
-        group_w2(1, nc.vector.tensor_copy)
         quantise_w2(1, 1)
-        split_w2(0, nc.scalar.copy)
-        turn_w2(0)
         planar0 = hidden_tile()
         for t in range(TILES):
             hidden_out_of_psum(acc0[t][:], planar0[:, t, :], 0, t)
+        quantise_w2(0, 1)
 
         planar1 = hidden_tile()
         for t in range(TILES):
@@ -297,13 +327,10 @@ def tile_qmlp_kernel(
             for c in range(PARTS):
                 layer1_pass(acc[:], 1, t, c, ALL_COLS, c == 0, c == PARTS - 1)
             hidden_out_of_psum(acc[:], planar1[:, t, :], 1, t)
-            if t == 0:
-                split_w2(3, nc.scalar.copy)
             if t == 1:
-                group_w2(0, nc.scalar.copy)
+                split_w2(3, nc.scalar.copy)
         quantise_hidden(planar0, 0, ALL_COLS)
         turn_w2(3)
-        quantise_w2(0, 1)
         quantise_hidden(planar1, 1, ALL_COLS)
 
         planar2 = hidden_tile()
@@ -338,7 +365,6 @@ def tile_qmlp_kernel(
         for half in range(2):
             for o in (1, 2, 0, 3):
                 for a in (2 * half, 2 * half + 1):
-                    acc = psum.tile([P, SIZE], F32, name="acc2", tag="bank")
-                    for c in range(PARTS):
-                        layer2_pass(acc, a, o, c, c == 0, c == PARTS - 1)
-                    store_output(acc, a, o)
+                    last = half == 1 and o == 3 and a == TILES - 1
+                    for features in (first, second) if last else (ALL_COLS,):
+                        output_tile(a, o, features)

@@ -80,7 +80,7 @@ def tile_qmlp_kernel(
                 out=b1_sb[:, c, 0:TILES],
                 in_=b1[c].rearrange("(p t) -> p t", t=TILES),
             )
-        w2_raw = {w: load("w2_raw%d" % w, w2[w].rearrange("(a p) k -> p a k", p=P)) for w in (1, 0)}
+        w2_raw = {1: load("w2_raw1", w2[1].rearrange("(a p) k -> p a k", p=P))}
 
         def load_w2_blocks(c):
             raw = raw_pool.tile([P, TILES * SIZE], BF16, name="w2_raw%d" % c)
@@ -91,7 +91,7 @@ def tile_qmlp_kernel(
                 )
             return raw
 
-        for w in (3, 2):
+        for w in (0, 3, 2):
             w2_raw[w] = load_w2_blocks(w)
         b2_sb = const.tile([P, PARTS, SIZE], BF16, name="b2_sb")
         for c in range(PARTS):
@@ -204,12 +204,8 @@ def tile_qmlp_kernel(
                 h_mx[o] = mx_operand("h%d" % o)
             quantise_into(h_mx[o], rows, grouped[:, 0 : count * PACK])
 
-        def output_tile(a, o, features):
-            width = features.stop - features.start
-            acc = psum.tile([P, width], F32, name="acc2", tag="bank")
-            for c in range(PARTS):
-                layer2_pass(acc[:], a, o, c, features, c == 0, c == PARTS - 1)
-            result = result_pool.tile([P, width], F32, name="result", tag="result")
+        def store_output(acc, a, o, features):
+            result = result_pool.tile([P, features.stop - features.start], F32, name="result", tag="result")
             bias = b2_sb[:, o, features]
             if FLIP[o] > 0:
                 nc.vector.tensor_tensor(
@@ -308,17 +304,17 @@ def tile_qmlp_kernel(
         layer1_term(acc0, 0, 2)
         layer1_term(acc0, 0, 3)
         split_w2(1, nc.scalar.copy)
-        split_w2(0, nc.scalar.copy)
-        transpose_w2(1)
         quantise_w1(0, -1)
         quantise_q(0)
         layer1_term(acc0, 0, 0, stop=True)
-        transpose_w2(0)
         quantise_w1(0, 1)
-        quantise_w2(1, 1)
         planar0 = hidden_tile()
         for t in range(TILES):
             hidden_out_of_psum(acc0[t][:], planar0[:, t, :], 0, t)
+        transpose_w2(1)
+        split_w2(0, nc.vector.tensor_copy)
+        turn_w2(0)
+        group_w2(0, nc.vector.tensor_copy)
         quantise_w2(0, 1)
 
         planar1 = hidden_tile()
@@ -330,6 +326,7 @@ def tile_qmlp_kernel(
             if t == 1:
                 split_w2(3, nc.scalar.copy)
         quantise_hidden(planar0, 0, ALL_COLS)
+        quantise_w2(1, 1)
         turn_w2(3)
         quantise_hidden(planar1, 1, ALL_COLS)
 
@@ -362,9 +359,27 @@ def tile_qmlp_kernel(
         quantise_hidden(planar2, 2, second)
         quantise_hidden(planar3, 3, second)
 
-        for half in range(2):
+        acc2 = {
+            (o, a): psum.tile([P, SIZE], F32, name="acc2_%d%d" % (o, a), tag="bank")
+            for o in range(PARTS)
+            for a in range(2)
+        }
+        todo = {o: PARTS for o in range(PARTS)}
+        for variant in ((1, 1), (0, 1), (3, 1), (2, -1), (2, 1), (3, -1), (0, -1)):
             for o in (1, 2, 0, 3):
-                for a in (2 * half, 2 * half + 1):
-                    last = half == 1 and o == 3 and a == TILES - 1
-                    for features in (first, second) if last else (ALL_COLS,):
-                        output_tile(a, o, features)
+                if variant in SIGNED[o]:
+                    c = SIGNED[o].index(variant)
+                    for a in range(2):
+                        layer2_pass(acc2[o, a][:], a, o, c, ALL_COLS, todo[o] == PARTS, todo[o] == 1)
+                    todo[o] -= 1
+                    if todo[o] == 0:
+                        for a in range(2):
+                            store_output(acc2[o, a], a, o, ALL_COLS)
+        for o in (1, 2, 0, 3):
+            for a in range(2, TILES):
+                last = o == 3 and a == TILES - 1
+                for features in (first, second) if last else (ALL_COLS,):
+                    acc = psum.tile([P, features.stop - features.start], F32, name="acc3", tag="bank")
+                    for c in range(PARTS):
+                        layer2_pass(acc[:], a, o, c, features, c == 0, c == PARTS - 1)
+                    store_output(acc, a, o, features)

@@ -99,6 +99,8 @@ def tile_qmlp_kernel(
 
         ident = const.tile([P, P], F32, name="ident")
         make_identity(nc, ident[:])
+        zeros = const.tile([P, SIZE], BF16, name="zeros")
+        nc.vector.memset(zeros[:], 0.0)
 
         def grouped_tile(name):
             return grouped_pool.tile(
@@ -225,8 +227,16 @@ def tile_qmlp_kernel(
         w2_turned = {}
         w2_grouped = {}
 
-        def transpose_pair(c):
+        idle_bank = psum.tile([P, SIZE], F32, name="idle_bank", tag="bank")
+
+        def keep_warm(count):
+            for i in range(count):
+                nc.tensor.matmul(idle_bank[:], zeros[:, 0:P], zeros[:], start=True, stop=True)
+
+        def transpose_w1(c):
             w1_grouped[c] = transpose_component(w1_raw[c], "w1_grouped%d" % c)
+
+        def transpose_q(c):
             q_grouped[c] = transpose_component(q_raw[c], "q_grouped%d" % c)
 
         def transpose_w2(w):
@@ -287,20 +297,36 @@ def tile_qmlp_kernel(
             else:
                 w2_mx[(w, 1)] = quantise(w2_grouped[w], "w2_plus%d" % w)
 
-        transpose_pair(1)
-        transpose_pair(2)
+        acc0 = []
+
+        def start_component_r(t):
+            acc0.append(psum.tile([P, SIZE], F32, name="acc0%d" % t, tag="bank"))
+            layer1_pass(acc0[t][:], 0, t, 1, ALL_COLS, True, False)
+
+        keep_warm(6)
+        transpose_w1(1)
+        keep_warm(1)
+        transpose_q(1)
+        keep_warm(1)
+        transpose_w1(2)
+        keep_warm(1)
+        transpose_q(2)
         quantise_w1(1, 1)
         quantise_q(1)
-        transpose_pair(3)
+        start_component_r(0)
+        transpose_w1(3)
         quantise_w1(2, 1)
         quantise_w1(2, -1)
+        start_component_r(1)
+        transpose_q(3)
         quantise_q(2)
-        transpose_pair(0)
+        start_component_r(2)
+        transpose_w1(0)
         quantise_w1(3, 1)
         quantise_w1(3, -1)
+        start_component_r(3)
+        transpose_q(0)
         quantise_q(3)
-        acc0 = four_banks("acc0")
-        layer1_term(acc0, 0, 1, start=True)
         layer1_term(acc0, 0, 2)
         layer1_term(acc0, 0, 3)
         split_w2(1, nc.scalar.copy)

@@ -169,6 +169,7 @@ def tile_qmlp_kernel(
         w1_mx = {}
         w2_mx = {}
         h_mx = {}
+        h_grouped = {}
 
         def four_banks(name):
             return [psum.tile([P, SIZE], F32, name="%s%d" % (name, t), tag="bank") for t in range(TILES)]
@@ -195,16 +196,20 @@ def tile_qmlp_kernel(
         def hidden_tile():
             return planar_pool.tile([P, TILES, SIZE], BF16, name="planar", tag="planar")
 
-        def quantise_hidden(planar, o, rows):
+        def group_hidden(planar, o, rows):
             grouped = grouped_tile("h_grouped%d" % o)
             count = rows.stop - rows.start
             nc.vector.tensor_copy(
                 out=grouped[:, 0 : count * PACK].rearrange("p (n i t) -> p n t i", i=4, t=PACK),
                 in_=planar[:, :, rows].rearrange("p t (n i) -> p n t i", i=4),
             )
+            h_grouped[o] = grouped
+
+        def quantise_hidden(o, rows):
             if o not in h_mx:
                 h_mx[o] = mx_operand("h%d" % o)
-            quantise_into(h_mx[o], rows, grouped[:, 0 : count * PACK])
+            count = rows.stop - rows.start
+            quantise_into(h_mx[o], rows, h_grouped[o][:, 0 : count * PACK])
 
         def store_output(acc, a, o, features):
             result = result_pool.tile([P, features.stop - features.start], F32, name="result", tag="result")
@@ -285,17 +290,22 @@ def tile_qmlp_kernel(
         def quantise_q(c):
             q_mx[c] = quantise(q_grouped[c], "q%d" % c)
 
+        def negate_w1(w):
+            w1_minus[w] = negate(w1_grouped[w], "w1_neg%d" % w)
+
+        def negate_w2(w):
+            w2_minus[w] = negate(w2_grouped[w], "w2_neg%d" % w)
+
         def quantise_w1(w, sign):
-            if sign < 0:
-                w1_mx[(w, -1)] = quantise(negate(w1_grouped[w], "w1_neg%d" % w), "w1_minus%d" % w)
-            else:
-                w1_mx[(w, 1)] = quantise(w1_grouped[w], "w1_plus%d" % w)
+            values = w1_grouped[w] if sign > 0 else w1_minus[w]
+            w1_mx[(w, sign)] = quantise(values, "w1_%d_%s" % (w, "plus" if sign > 0 else "minus"))
 
         def quantise_w2(w, sign):
-            if sign < 0:
-                w2_mx[(w, -1)] = quantise(negate(w2_grouped[w], "w2_neg%d" % w), "w2_minus%d" % w)
-            else:
-                w2_mx[(w, 1)] = quantise(w2_grouped[w], "w2_plus%d" % w)
+            values = w2_grouped[w] if sign > 0 else w2_minus[w]
+            w2_mx[(w, sign)] = quantise(values, "w2_%d_%s" % (w, "plus" if sign > 0 else "minus"))
+
+        w1_minus = {}
+        w2_minus = {}
 
         acc0 = []
 
@@ -315,6 +325,7 @@ def tile_qmlp_kernel(
         quantise_q(1)
         start_component_r(0)
         transpose_w1(3)
+        negate_w1(2)
         quantise_w1(2, 1)
         quantise_w1(2, -1)
         start_component_r(1)
@@ -322,6 +333,7 @@ def tile_qmlp_kernel(
         quantise_q(2)
         start_component_r(2)
         transpose_w1(0)
+        negate_w1(3)
         quantise_w1(3, 1)
         quantise_w1(3, -1)
         start_component_r(3)
@@ -330,10 +342,11 @@ def tile_qmlp_kernel(
         layer1_term(acc0, 0, 2)
         layer1_term(acc0, 0, 3)
         split_w2(1, nc.scalar.copy)
+        negate_w1(0)
+        quantise_w1(0, 1)
         quantise_w1(0, -1)
         quantise_q(0)
         layer1_term(acc0, 0, 0, stop=True)
-        quantise_w1(0, 1)
         planar0 = hidden_tile()
         for t in range(TILES):
             hidden_out_of_psum(acc0[t][:], planar0[:, t, :], 0, t)
@@ -341,7 +354,6 @@ def tile_qmlp_kernel(
         split_w2(0, nc.vector.tensor_copy)
         turn_w2(0)
         group_w2(0, nc.vector.tensor_copy)
-        quantise_w2(0, 1)
 
         planar1 = hidden_tile()
         for t in range(TILES):
@@ -351,10 +363,13 @@ def tile_qmlp_kernel(
             hidden_out_of_psum(acc[:], planar1[:, t, :], 1, t)
             if t == 1:
                 split_w2(3, nc.scalar.copy)
-        quantise_hidden(planar0, 0, ALL_COLS)
-        quantise_w2(1, 1)
+        group_hidden(planar0, 0, ALL_COLS)
+        quantise_w2(0, 1)
+        quantise_hidden(0, ALL_COLS)
         turn_w2(3)
-        quantise_hidden(planar1, 1, ALL_COLS)
+        group_hidden(planar1, 1, ALL_COLS)
+        quantise_w2(1, 1)
+        quantise_hidden(1, ALL_COLS)
 
         planar2 = hidden_tile()
         planar3 = hidden_tile()
@@ -370,20 +385,27 @@ def tile_qmlp_kernel(
 
         first, second = slice(0, HALF), slice(HALF, SIZE)
         layer1_half(2, planar2, first, lambda: split_w2(2, nc.scalar.copy))
-        quantise_hidden(planar2, 2, first)
+        group_hidden(planar2, 2, first)
         turn_w2(2)
+        quantise_hidden(2, first)
         layer1_half(3, planar3, first, lambda: group_w2(3, nc.scalar.copy))
-        quantise_hidden(planar3, 3, first)
-        group_w2(2, nc.scalar.copy)
+        group_hidden(planar3, 3, first)
         quantise_w2(3, 1)
-        quantise_w2(2, -1)
+        quantise_hidden(3, first)
+        group_w2(2, nc.scalar.copy)
+        negate_w2(2)
         quantise_w2(2, 1)
+        quantise_w2(2, -1)
+        negate_w2(3)
+        negate_w2(0)
         quantise_w2(3, -1)
+        quantise_w2(0, -1)
         layer1_half(2, planar2, second)
         layer1_half(3, planar3, second)
-        quantise_w2(0, -1)
-        quantise_hidden(planar2, 2, second)
-        quantise_hidden(planar3, 3, second)
+        group_hidden(planar2, 2, second)
+        group_hidden(planar3, 3, second)
+        quantise_hidden(2, second)
+        quantise_hidden(3, second)
 
         acc2 = {
             (o, a): psum.tile([P, SIZE], F32, name="acc2_%d%d" % (o, a), tag="bank")
@@ -391,7 +413,7 @@ def tile_qmlp_kernel(
             for a in range(2)
         }
         todo = {o: PARTS for o in range(PARTS)}
-        for variant in ((1, 1), (0, 1), (3, 1), (2, -1), (2, 1), (3, -1), (0, -1)):
+        for variant in ((1, 1), (0, 1), (3, 1), (2, 1), (2, -1), (3, -1), (0, -1)):
             for o in (1, 2, 0, 3):
                 if variant in SIGNED[o]:
                     c = SIGNED[o].index(variant)

@@ -313,7 +313,7 @@ def tile_qmlp_kernel(
             acc0.append(psum.tile([P, SIZE], F32, name="acc0%d" % t, tag="bank"))
             layer1_pass(acc0[t][:], 0, t, 1, ALL_COLS, True, False)
 
-        keep_warm(6)
+        keep_warm(4)
         transpose_w1(1)
         keep_warm(1)
         transpose_q(1)
@@ -392,15 +392,15 @@ def tile_qmlp_kernel(
         group_hidden(planar3, 3, first)
         quantise_w2(3, 1)
         quantise_hidden(3, first)
+        negate_w2(3)
+        negate_w2(0)
+        layer1_half(2, planar2, second)
         group_w2(2, nc.scalar.copy)
+        quantise_w2(3, -1)
+        quantise_w2(0, -1)
         negate_w2(2)
         quantise_w2(2, 1)
         quantise_w2(2, -1)
-        negate_w2(3)
-        negate_w2(0)
-        quantise_w2(3, -1)
-        quantise_w2(0, -1)
-        layer1_half(2, planar2, second)
         layer1_half(3, planar3, second)
         group_hidden(planar2, 2, second)
         group_hidden(planar3, 3, second)
@@ -413,7 +413,7 @@ def tile_qmlp_kernel(
             for a in range(2)
         }
         todo = {o: PARTS for o in range(PARTS)}
-        for variant in ((1, 1), (0, 1), (3, 1), (2, 1), (2, -1), (3, -1), (0, -1)):
+        for variant in ((1, 1), (0, 1), (3, 1), (3, -1), (0, -1), (2, 1), (2, -1)):
             for o in (1, 2, 0, 3):
                 if variant in SIGNED[o]:
                     c = SIGNED[o].index(variant)

@@ -136,8 +136,8 @@ def tile_qmlp_kernel(
             return minus
 
         def mx_operand(name):
-            codes = mx_pool.tile([P, SIZE], U32, name=name + "_codes", align_bytes=64)
-            scales = mx_pool.tile([P, SIZE], U8, name=name + "_scales", align_bytes=64)
+            codes = mx_pool.tile([P, SIZE], U32, name=name + "_codes", align_bytes=256)
+            scales = mx_pool.tile([P, SIZE], U8, name=name + "_scales", align_bytes=256)
             return codes, scales
 
         def quantise_into(operand, cols, values):

from contextlib import ExitStack

import concourse.mybir as mybir
from concourse.masks import make_identity

F32 = mybir.dt.float32
BF16 = mybir.dt.bfloat16
U32 = mybir.dt.uint32
U8 = mybir.dt.uint8
FP8X4 = mybir.dt.float8_e4m3fn_x4

P = 128
SIZE = 512
TILES = SIZE // P
PACK = 4
PARTS = 4
HALF = SIZE // 2
BLOCK = 32

FLOPS = 2 * 2 * SIZE * (PARTS * SIZE) * (PARTS * SIZE)

SIGNED = (
    ((0, -1), (1, 1), (2, 1), (3, 1)),
    ((1, 1), (0, 1), (3, 1), (2, -1)),
    ((2, 1), (3, -1), (0, 1), (1, 1)),
    ((3, -1), (2, -1), (1, 1), (0, -1)),
)
FLIP = (-1, 1, 1, -1)

ALL_COLS = slice(0, SIZE)


def tile_qmlp_kernel(
    tc,
    q_r, q_i, q_j, q_k,
    W1_r, W1_i, W1_j, W1_k,
    b1_r, b1_i, b1_j, b1_k,
    W2_r, W2_i, W2_j, W2_k,
    b2_r, b2_i, b2_j, b2_k,
    out_0, out_1, out_2, out_3,
):
    nc = tc.nc
    q = (q_r, q_i, q_j, q_k)
    w1 = (W1_r, W1_i, W1_j, W1_k)
    b1 = (b1_r, b1_i, b1_j, b1_k)
    w2 = (W2_r, W2_i, W2_j, W2_k)
    b2 = (b2_r, b2_i, b2_j, b2_k)
    outs = (out_0, out_1, out_2, out_3)

    with ExitStack() as ctx:
        const = ctx.enter_context(tc.tile_pool(name="const", bufs=1))
        raw_pool = ctx.enter_context(tc.tile_pool(name="raw", bufs=1))
        grouped_pool = ctx.enter_context(tc.tile_pool(name="grouped", bufs=10))
        planar_pool = ctx.enter_context(tc.tile_pool(name="planar", bufs=4))
        w2_pool = ctx.enter_context(tc.tile_pool(name="w2", bufs=2))
        mx_pool = ctx.enter_context(tc.tile_pool(name="mx", bufs=1))
        result_pool = ctx.enter_context(tc.tile_pool(name="result", bufs=8))
        psum = ctx.enter_context(tc.psum_pool(name="psum", bufs=8))
        ctx.enter_context(tc.manual_schedule())

        def load(name, view, pieces=1):
            raw = raw_pool.tile([P, TILES * SIZE], BF16, name=name)
            tiles = TILES // pieces
            for n in range(0, TILES, tiles):
                nc.sync.dma_start(
                    out=raw[:].rearrange("p (n x) -> p n x", n=TILES)[:, n : n + tiles, :],
                    in_=view[:, n : n + tiles, :],
                )
            return raw

        q_raw = {}
        w1_raw = {}
        for c in (1, 2, 3, 0):
            pieces = 2 if c in (1, 0) else 1
            w1_raw[c] = load("w1_raw%d" % c, w1[c].rearrange("(p t) k -> p t k", t=TILES), pieces)
            q_raw[c] = load("q_raw%d" % c, q[c].rearrange("(p a) k -> p a k", a=TILES), pieces)
        b1_sb = const.tile([P, PARTS, 16], BF16, name="b1_sb")
        for c in range(PARTS):
            nc.sync.dma_start(
                out=b1_sb[:, c, 0:TILES],
                in_=b1[c].rearrange("(p t) -> p t", t=TILES),
            )
        w2_raw = {1: load("w2_raw1", w2[1].rearrange("(a p) k -> p a k", p=P))}

        def load_w2_blocks(c):
            raw = raw_pool.tile([P, TILES * SIZE], BF16, name="w2_raw%d" % c)
            for Q in range(P // BLOCK):
                nc.sync.dma_start(
                    out=raw[Q * BLOCK : (Q + 1) * BLOCK, :].rearrange("j (b k) -> j b k", k=P),
                    in_=w2[c].rearrange("(b j) k -> j b k", j=BLOCK)[:, :, Q * P : (Q + 1) * P],
                )
            return raw

        for w in (0, 3, 2):
            w2_raw[w] = load_w2_blocks(w)
        b2_sb = const.tile([P, PARTS, SIZE], BF16, name="b2_sb")
        for c in range(PARTS):
            nc.sync.dma_start(out=b2_sb[:, c, :], in_=b2[c].partition_broadcast(P))

        ident = const.tile([P, P], F32, name="ident")
        make_identity(nc, ident[:])
        zeros = const.tile([P, SIZE], BF16, name="zeros")
        nc.vector.memset(zeros[:], 0.0)

        def grouped_tile(name):
            return grouped_pool.tile(
                [P, SIZE * PACK], BF16, name=name, tag="grouped", align_bytes=64
            )

        def transpose_component(raw, name):
            words = raw[:].bitcast(F32)
            grouped = grouped_tile(name)
            grouped_words = grouped[:].bitcast(F32)
            half = SIZE
            for b in range(2):
                bank = psum.tile([P, SIZE], F32, name="%s_bank%d" % (name, b), tag="bank")
                for u in range(2):
                    for a2 in range(2):
                        start = (2 * b + a2) * 2 * P
                        nc.tensor.transpose(
                            bank[:, (2 * u + a2) * P : (2 * u + a2 + 1) * P],
                            words[:, start + u : start + 2 * P : 2],
                            ident[:],
                        )
                nc.scalar.copy(
                    out=grouped_words[:, b * half : (b + 1) * half].rearrange(
                        "p (n u) -> p n u", u=2
                    ),
                    in_=bank[:].rearrange("p (u n) -> p n u", u=2),
                )
            return grouped

        def negate(grouped, name):
            minus = grouped_tile(name)
            nc.vector.tensor_scalar_mul(out=minus[:], in0=grouped[:], scalar1=-1.0)
            return minus

        def mx_operand(name):
            codes = mx_pool.tile([P, SIZE], U32, name=name + "_codes", align_bytes=256)
            scales = mx_pool.tile([P, SIZE], U8, name=name + "_scales", align_bytes=256)
            return codes, scales

        def quantise_into(operand, cols, values):
            codes, scales = operand
            nc.vector.quantize_mx(
                out=codes[:, cols].bitcast(FP8X4), scales=scales[:, cols], in_=values
            )

        def quantise(grouped, name):
            operand = mx_operand(name)
            quantise_into(operand, ALL_COLS, grouped[:])
            return operand

        def mx_pass(acc, stationary, tile_index, moving, moving_cols, start, stop):
            s_codes, s_scales = stationary
            m_codes, m_scales = moving
            cols = slice(tile_index * P, (tile_index + 1) * P)
            nc.tensor.matmul_mx(
                out=acc,
                lhsT=s_codes[:, cols].bitcast(FP8X4),
                lhsT_scale=s_scales[:, cols],
                rhs=m_codes[:, moving_cols].bitcast(FP8X4),
                rhs_scale=m_scales[:, moving_cols],
                start=start,
                stop=stop,
            )

        q_mx = {}
        w1_mx = {}
        w2_mx = {}
        h_mx = {}
        h_grouped = {}

        def four_banks(name):
            return [psum.tile([P, SIZE], F32, name="%s%d" % (name, t), tag="bank") for t in range(TILES)]

        def layer1_pass(acc, o, t, c, rows, start, stop):
            mx_pass(acc, w1_mx[SIGNED[o][c]], t, q_mx[c], rows, start, stop)

        def layer1_term(acc, o, c, start=False, stop=False):
            for t in range(TILES):
                layer1_pass(acc[t][:], o, t, c, ALL_COLS, start, stop)

        def layer2_pass(acc, a, o, c, features, start, stop):
            mx_pass(acc, h_mx[c], a, w2_mx[SIGNED[o][c]], features, start, stop)

        def hidden_out_of_psum(acc, planar, o, t):
            nc.scalar.activation(
                out=planar,
                in_=acc,
                func=mybir.ActivationFunctionType.Relu,
                bias=b1_sb[:, o, t : t + 1],
                scale=float(FLIP[o]),
            )

        def hidden_tile():
            return planar_pool.tile([P, TILES, SIZE], BF16, name="planar", tag="planar")

        def group_hidden(planar, o, rows):
            grouped = grouped_tile("h_grouped%d" % o)
            count = rows.stop - rows.start
            nc.vector.tensor_copy(
                out=grouped[:, 0 : count * PACK].rearrange("p (n i t) -> p n t i", i=4, t=PACK),
                in_=planar[:, :, rows].rearrange("p t (n i) -> p n t i", i=4),
            )
            h_grouped[o] = grouped

        def quantise_hidden(o, rows):
            if o not in h_mx:
                h_mx[o] = mx_operand("h%d" % o)
            count = rows.stop - rows.start
            quantise_into(h_mx[o], rows, h_grouped[o][:, 0 : count * PACK])

        def store_output(acc, a, o, features):
            result = result_pool.tile([P, features.stop - features.start], F32, name="result", tag="result")
            bias = b2_sb[:, o, features]
            if FLIP[o] > 0:
                nc.vector.tensor_tensor(
                    out=result[:], in0=acc[:], in1=bias, op=mybir.AluOpType.add
                )
            else:
                nc.vector.tensor_tensor(
                    out=result[:], in0=bias, in1=acc[:], op=mybir.AluOpType.subtract
                )
            nc.sync.dma_start(
                out=outs[o].rearrange("(p a) n -> p a n", a=TILES)[:, a, features], in_=result[:]
            )

        q_grouped = {}
        w1_grouped = {}
        w2_split = {}
        w2_turned = {}
        w2_grouped = {}

        idle_bank = psum.tile([P, SIZE], F32, name="idle_bank", tag="bank")

        def keep_warm(count):
            for i in range(count):
                nc.tensor.matmul(idle_bank[:], zeros[:, 0:P], zeros[:], start=True, stop=True)

        def transpose_w1(c):
            w1_grouped[c] = transpose_component(w1_raw[c], "w1_grouped%d" % c)

        def transpose_q(c):
            q_grouped[c] = transpose_component(q_raw[c], "q_grouped%d" % c)

        def transpose_w2(w):
            words = w2_split[w][:].bitcast(F32)
            grouped = grouped_tile("w2_grouped%d" % w)
            grouped_words = grouped[:].bitcast(F32)
            for b in range(2):
                bank = psum.tile([P, SIZE], F32, name="w2_bank", tag="bank")
                for u in range(2):
                    for a2 in range(2):
                        start = u * SIZE + (2 * b + a2) * P
                        nc.tensor.transpose(
                            bank[:, (2 * u + a2) * P : (2 * u + a2 + 1) * P],
                            words[:, start : start + P],
                            ident[:],
                        )
                nc.scalar.copy(
                    out=grouped_words[:, b * SIZE : (b + 1) * SIZE].rearrange(
                        "p (n u) -> p n u", u=2
                    ),
                    in_=bank[:].rearrange("p (u n) -> p n u", u=2),
                )
            w2_grouped[w] = grouped

        def split_w2(w, copy):
            split = w2_pool.tile([P, TILES * SIZE], BF16, name="split", align_bytes=64)
            copy(
                out=split[:].bitcast(F32).rearrange("p (v m) -> p v m", v=2),
                in_=w2_raw[w][:].bitcast(F32).rearrange("p (m v) -> p v m", v=2),
            )
            w2_split[w] = split

        def turn_w2(w):
            turned = w2_pool.tile([P, TILES * SIZE], BF16, name="turned", align_bytes=64)
            nc.vector.transpose(out=turned[:].bitcast(F32), in_=w2_split[w][:].bitcast(F32))
            w2_turned[w] = turned

        def group_w2(w, copy):
            grouped = grouped_tile("w2_grouped%d" % w)
            copy(
                out=grouped[:].bitcast(F32).rearrange("p (n v) -> p n v", v=2),
                in_=w2_turned[w][:].bitcast(F32).rearrange("p (v n) -> p n v", v=2),
            )
            w2_grouped[w] = grouped

        def quantise_q(c):
            q_mx[c] = quantise(q_grouped[c], "q%d" % c)

        def negate_w1(w):
            w1_minus[w] = negate(w1_grouped[w], "w1_neg%d" % w)

        def negate_w2(w):
            w2_minus[w] = negate(w2_grouped[w], "w2_neg%d" % w)

        def quantise_w1(w, sign):
            values = w1_grouped[w] if sign > 0 else w1_minus[w]
            w1_mx[(w, sign)] = quantise(values, "w1_%d_%s" % (w, "plus" if sign > 0 else "minus"))

        def quantise_w2(w, sign):
            values = w2_grouped[w] if sign > 0 else w2_minus[w]
            w2_mx[(w, sign)] = quantise(values, "w2_%d_%s" % (w, "plus" if sign > 0 else "minus"))

        w1_minus = {}
        w2_minus = {}

        acc0 = []

        def start_component_r(t):
            acc0.append(psum.tile([P, SIZE], F32, name="acc0%d" % t, tag="bank"))
            layer1_pass(acc0[t][:], 0, t, 1, ALL_COLS, True, False)

        keep_warm(4)
        transpose_w1(1)
        keep_warm(1)
        transpose_q(1)
        keep_warm(1)
        transpose_w1(2)
        keep_warm(1)
        transpose_q(2)
        quantise_w1(1, 1)
        quantise_q(1)
        start_component_r(0)
        transpose_w1(3)
        negate_w1(2)
        quantise_w1(2, 1)
        quantise_w1(2, -1)
        start_component_r(1)
        transpose_q(3)
        quantise_q(2)
        start_component_r(2)
        transpose_w1(0)
        negate_w1(3)
        quantise_w1(3, 1)
        quantise_w1(3, -1)
        start_component_r(3)
        transpose_q(0)
        quantise_q(3)
        layer1_term(acc0, 0, 2)
        layer1_term(acc0, 0, 3)
        split_w2(1, nc.scalar.copy)
        negate_w1(0)
        quantise_w1(0, 1)
        quantise_w1(0, -1)
        quantise_q(0)
        layer1_term(acc0, 0, 0, stop=True)
        planar0 = hidden_tile()
        for t in range(TILES):
            hidden_out_of_psum(acc0[t][:], planar0[:, t, :], 0, t)
        transpose_w2(1)
        split_w2(0, nc.vector.tensor_copy)
        turn_w2(0)
        group_w2(0, nc.vector.tensor_copy)

        planar1 = hidden_tile()
        for t in range(TILES):
            acc = psum.tile([P, SIZE], F32, name="acc1", tag="bank")
            for c in range(PARTS):
                layer1_pass(acc[:], 1, t, c, ALL_COLS, c == 0, c == PARTS - 1)
            hidden_out_of_psum(acc[:], planar1[:, t, :], 1, t)
            if t == 1:
                split_w2(3, nc.scalar.copy)
        group_hidden(planar0, 0, ALL_COLS)
        quantise_w2(0, 1)
        quantise_hidden(0, ALL_COLS)
        turn_w2(3)
        group_hidden(planar1, 1, ALL_COLS)
        quantise_w2(1, 1)
        quantise_hidden(1, ALL_COLS)

        planar2 = hidden_tile()
        planar3 = hidden_tile()

        def layer1_half(o, planar, rows, scalar_step=None):
            for t in range(TILES):
                acc = psum.tile([P, HALF], F32, name="acc_half", tag="bank")
                for c in range(PARTS):
                    layer1_pass(acc[:], o, t, c, rows, c == 0, c == PARTS - 1)
                hidden_out_of_psum(acc[:], planar[:, t, rows], o, t)
                if t == 1 and scalar_step:
                    scalar_step()

        first, second = slice(0, HALF), slice(HALF, SIZE)
        layer1_half(2, planar2, first, lambda: split_w2(2, nc.scalar.copy))
        group_hidden(planar2, 2, first)
        turn_w2(2)
        quantise_hidden(2, first)
        layer1_half(3, planar3, first, lambda: group_w2(3, nc.scalar.copy))
        group_hidden(planar3, 3, first)
        quantise_w2(3, 1)
        quantise_hidden(3, first)
        negate_w2(3)
        negate_w2(0)
        layer1_half(2, planar2, second)
        group_w2(2, nc.scalar.copy)
        quantise_w2(3, -1)
        quantise_w2(0, -1)
        negate_w2(2)
        quantise_w2(2, 1)
        quantise_w2(2, -1)
        layer1_half(3, planar3, second)
        group_hidden(planar2, 2, second)
        group_hidden(planar3, 3, second)
        quantise_hidden(2, second)
        quantise_hidden(3, second)

        acc2 = {
            (o, a): psum.tile([P, SIZE], F32, name="acc2_%d%d" % (o, a), tag="bank")
            for o in range(PARTS)
            for a in range(2)
        }
        todo = {o: PARTS for o in range(PARTS)}
        for variant in ((1, 1), (0, 1), (3, 1), (3, -1), (0, -1), (2, 1), (2, -1)):
            for o in (1, 2, 0, 3):
                if variant in SIGNED[o]:
                    c = SIGNED[o].index(variant)
                    for a in range(2):
                        layer2_pass(acc2[o, a][:], a, o, c, ALL_COLS, todo[o] == PARTS, todo[o] == 1)
                    todo[o] -= 1
                    if todo[o] == 0:
                        for a in range(2):
                            store_output(acc2[o, a], a, o, ALL_COLS)
        for o in (1, 2, 0, 3):
            for a in range(2, TILES):
                last = o == 3 and a == TILES - 1
                for features in (first, second) if last else (ALL_COLS,):
                    acc = psum.tile([P, features.stop - features.start], F32, name="acc3", tag="bank")
                    for c in range(PARTS):
                        layer2_pass(acc[:], a, o, c, features, c == 0, c == PARTS - 1)
                    store_output(acc, a, o, features)
